import numpy as np
import ml_dtypes


def mxq(x, axis, fmt="e4m3"):
    dtype, down = {"e4m3": (ml_dtypes.float8_e4m3fn, 7), "e5m2": (ml_dtypes.float8_e5m2, 14)}[fmt]
    v = np.moveaxis(np.asarray(x, np.float32).astype(ml_dtypes.bfloat16).astype(np.float64), axis, -1)
    blocks = v.reshape(v.shape[:-1] + (-1, 32))
    amax = np.abs(blocks).max(-1, keepdims=True)
    byte = np.maximum(np.where(amax > 0, np.frexp(amax)[1] - 1 + 127, 0) - down, 1)
    scale = np.exp2(byte - 127.0)
    codes = (blocks / scale).astype(np.float32).astype(dtype).astype(np.float64)
    return np.moveaxis((codes * scale).reshape(v.shape), -1, axis)


WIDE = False


def mx_kscale(k):
    if not WIDE:
        return np.ones(k)
    levels = np.array([10, -10, 5, -5, 0])
    a = np.random.permutation(np.resize(levels, k // 512 * 4)).reshape(k // 512, 4)
    idx = np.arange(k)
    return np.exp2(a[idx // 512, idx % 128 // 32])


BF16 = ml_dtypes.bfloat16


def bf(x):
    return np.asarray(x, np.float32).astype(BF16)


def f64(x):
    return np.asarray(x).astype(np.float64)


E2M1 = np.array([0.0, 0.5, 1.0, 1.5, 2.0, 3.0, 4.0, 6.0, -0.0, -0.5, -1.0, -1.5, -2.0, -3.0, -4.0, -6.0])


def pack_weight(w, fmt):
    k, n = w.shape
    w = f64(bf(w)).reshape(k // 32, 32, n)
    amax = np.abs(w).max(1)
    if fmt == "e4m3":
        byte = np.frexp(amax)[1] - 1 + 127 - 7
    else:
        mant, ex = np.frexp(amax / 6.0)
        byte = np.where(mant > 0.5, ex, ex - 1) + 127
    byte = np.clip(np.where(amax > 0, byte, 1), 1, 254)
    scaled = (w * np.exp2(127.0 - byte)[:, None, :]).reshape(k, n).astype(np.float32)
    by_word = np.ascontiguousarray(scaled.reshape(k // 512, 128, 4, n).transpose(0, 1, 3, 2))
    if fmt == "e4m3":
        words = by_word.astype(ml_dtypes.float8_e4m3fn).view(np.uint8)
    else:
        c = by_word.astype(ml_dtypes.float4_e2m1fn).view(np.uint8) & 0xF
        words = c[..., 0::2] | (c[..., 1::2] << 4)
    return np.ascontiguousarray(words), np.ascontiguousarray(byte.astype(np.uint8).reshape(k // 512, 16, n))


def unpack_weight(words, scales, fmt):
    g, p, n, _ = words.shape
    if fmt == "e4m3":
        vals = np.ascontiguousarray(words).view(ml_dtypes.float8_e4m3fn).astype(np.float64)
    else:
        nib = np.empty((g, p, n, 4), np.uint8)
        nib[..., 0::2] = words & 0xF
        nib[..., 1::2] = words >> 4
        vals = E2M1[nib]
    vals = vals * np.repeat(np.exp2(scales.astype(np.float64) - 127.0), 8, axis=1)[..., None]
    return vals.transpose(0, 1, 3, 2).reshape(g * 512, n)


B, NE, D, H = 1, 128, 2560, 20
HD = D // H
LN_EPS = 1e-5
FMT = "e4m3"


def setup_inputs():
    s = mx_kscale(D)
    r = np.exp2(-8.0 * np.random.random_sample((B, NE, 1)))
    inp = bf((np.random.standard_normal((B, NE, D)) + 0.5) * r)
    gamma = bf((1.0 + 0.1 * np.random.standard_normal(D)) * s)
    beta = bf(0.1 * np.random.standard_normal(D) * s)
    W_qk_words, W_qk_scales = pack_weight(np.random.standard_normal((D, 2 * D)) / np.sqrt(D) / s[:, None], FMT)
    b_qk = bf(0.1 * np.random.standard_normal(2 * D))
    W_v_words, W_v_scales = pack_weight(np.random.standard_normal((D, D)) / np.sqrt(D) / s[:, None], FMT)
    b_v = bf(0.1 * np.random.standard_normal(D))
    return {
        "inp": inp,
        "gamma": gamma,
        "beta": beta,
        "W_qk_words": W_qk_words,
        "W_qk_scales": W_qk_scales,
        "b_qk": b_qk,
        "W_v_words": W_v_words,
        "W_v_scales": W_v_scales,
        "b_v": b_v,
    }


def reference(inp, gamma, beta, W_qk_words, W_qk_scales, b_qk, W_v_words, W_v_scales, b_v):
    inp = f64(inp)
    mu = np.mean(inp, axis=-1, keepdims=True)
    var = np.mean(np.square(inp - mu), axis=-1, keepdims=True)
    x = (inp - mu) / np.sqrt(var + LN_EPS) * f64(gamma) + f64(beta)
    xq = mxq(x, 2, "e4m3")
    qk = ((xq @ unpack_weight(W_qk_words, W_qk_scales, FMT)) + f64(b_qk)).reshape(B, NE, H, HD, 2)
    q = qk[..., 0]
    k = qk[..., 1]
    v = ((xq @ unpack_weight(W_v_words, W_v_scales, FMT)) + f64(b_v)).reshape(B, NE, H, HD)
    q = np.transpose(q, (0, 2, 1, 3))
    k = np.transpose(k, (0, 2, 3, 1))
    v = np.transpose(v, (0, 2, 1, 3))
    return (q, k, v)

@@ -1,0 +1,215 @@
+from contextlib import ExitStack
+
+import concourse.mybir as mybir
+from concourse.masks import make_identity
+
+F32 = mybir.dt.float32
+BF16 = mybir.dt.bfloat16
+I32 = mybir.dt.int32
+U32 = mybir.dt.uint32
+U8 = mybir.dt.uint8
+FP8X4 = mybir.dt.float8_e4m3fn_x4
+ALU = mybir.AluOpType
+ACT = mybir.ActivationFunctionType
+
+P = 128
+D = 2560
+G = 5
+NB = 512
+RW = 2560
+BANKS = RW // NB
+LN_EPS = 1e-5
+FLOPS = 2 * 128 * 2560 * 7680
+SCALES_ON_GPSIMD = False
+
+
+def tile_relational_w_kernel(
+    tc, inp, gamma, beta, W_qk_words, W_qk_scales, b_qk, W_v_words, W_v_scales, b_v, out_0, out_1, out_2
+):
+    nc = tc.nc
+    with ExitStack() as ctx:
+        const = ctx.enter_context(tc.tile_pool(name="const", bufs=1))
+        wpool = ctx.enter_context(tc.tile_pool(name="wpool", bufs=1))
+        xpool = ctx.enter_context(tc.tile_pool(name="xpool", bufs=1))
+        opool = ctx.enter_context(tc.tile_pool(name="opool", bufs=1))
+        accp = ctx.enter_context(tc.psum_pool(name="accp", bufs=6))
+        auxp = ctx.enter_context(tc.psum_pool(name="auxp", bufs=2))
+
+        planes = wpool.tile([P, 4 * RW], U8, name="planes", align_bytes=64)
+        rows = const.tile([P, NB], BF16, name="rows")
+        warm = const.tile([P, 1], F32, name="warm")
+        ident_f = const.tile([P, P], F32, name="ident_f")
+        ident_b = const.tile([P, P], BF16, name="ident_b")
+        inp_sb = xpool.tile([P, D], BF16, name="inp_sb")
+        words = [[wpool.tile([P, RW], I32, name="w%d_%d" % (r, g), align_bytes=64) for g in range(G)] for r in range(3)]
+        q_sb = opool.tile([P, D], F32, name="q_sb")
+        v_sb = opool.tile([P, D], F32, name="v_sb")
+        ks = opool.tile([P, G, 4, P], F32, name="ks")
+        k2 = opool.tile([P, G, NB], F32, name="k2")
+
+        nc.vector.memset(planes[:].bitcast(I32), 0)
+        nc.vector.memset(rows[:], 0.0)
+        nc.vector.memset(warm[:], 1.0)
+        nc.scalar.sqrt(warm[:], warm[:])
+        make_identity(nc, ident_b[:])
+        make_identity(nc, ident_f[:])
+
+        nc.sync.dma_start(out=inp_sb[:], in_=inp[0])
+        nc.scalar.dma_start(out=rows[15:20, :], in_=gamma.rearrange("(r c) -> r c", c=NB))
+        nc.scalar.dma_start(out=rows[20:25, :], in_=beta.rearrange("(r c) -> r c", c=NB))
+        nc.scalar.dma_start(out=rows[0:10, :], in_=b_qk.rearrange("(r c) -> r c", c=NB))
+        nc.scalar.dma_start(out=rows[10:15, :], in_=b_v.rearrange("(r c) -> r c", c=NB))
+
+        def scale_dma(dst, src):
+            if SCALES_ON_GPSIMD:
+                nc.gpsimd.dma_start(out=dst.bitcast(F32), in_=src.bitcast(F32))
+            else:
+                nc.sync.dma_start(out=dst.bitcast(I32), in_=src.bitcast(I32))
+
+        for Q in range(4):
+            scale_dma(planes[32 * Q : 32 * Q + 16, 0 : 2 * RW], W_qk_scales[0:4, 4 * Q : 4 * Q + 4, :])
+        for Q in range(4):
+            scale_dma(
+                planes[32 * Q : 32 * Q + 8, 3 * RW : 4 * RW],
+                W_qk_scales[4, 4 * Q : 4 * Q + 4, :].rearrange("r (o c) -> o r c", o=2),
+            )
+        for Q in range(4):
+            scale_dma(planes[32 * Q : 32 * Q + 16, 2 * RW : 3 * RW], W_v_scales[0:4, 4 * Q : 4 * Q + 4, :])
+        for Q in range(4):
+            scale_dma(planes[32 * Q + 8 : 32 * Q + 12, 3 * RW : 4 * RW], W_v_scales[4, 4 * Q : 4 * Q + 4, :])
+
+        for r in range(3):
+            for g in range(G):
+                if r < 2:
+                    src = W_qk_words[g].rearrange("p n t -> p (n t)")[:, 4 * RW * r : 4 * RW * (r + 1)]
+                else:
+                    src = W_v_words[g].rearrange("p n t -> p (n t)")
+                nc.sync.dma_start(out=words[r][g][:], in_=src.bitcast(I32))
+
+        rows_s = const.tile([P, 4, P], BF16, name="rows_s")
+        nc.vector.tensor_copy(out=rows_s[:], in_=rows[:].rearrange("r (p t) -> r t p", t=4))
+        gb_ps = auxp.tile([P, 4, P], BF16, name="gb_ps", tag="aux")
+        for t in range(4):
+            nc.tensor.transpose(gb_ps[:, t, :], rows_s[:, t, :], ident_b[:])
+        gb = const.tile([P, 10, 4], F32, name="gb")
+        nc.vector.tensor_copy(out=gb[:], in_=gb_ps[:, :, 15:25].rearrange("p t j -> p j t"))
+
+        def bias_chunk(c):
+            pb = auxp.tile([P, NB], F32, name="pb", tag="aux")
+            nc.tensor.matmul(
+                pb[:], lhsT=ident_b[:, c : c + 1].to_broadcast([P, P]), rhs=rows[:], start=True, stop=True
+            )
+            if c < 10:
+                nc.scalar.copy(
+                    out=q_sb[:, 256 * c : 256 * (c + 1)],
+                    in_=pb[:].rearrange("n (i two) -> n two i", two=2)[:, 0, :],
+                )
+                nc.scalar.copy(
+                    out=ks[:, c // 2, :, 64 * (c % 2) : 64 * (c % 2) + 64],
+                    in_=pb[:].rearrange("n (pp e two) -> n two e pp", e=4, two=2)[:, 1],
+                )
+            else:
+                nc.scalar.copy(out=v_sb[:, NB * (c - 10) : NB * (c - 9)], in_=pb[:])
+
+        stats = xpool.tile([P, G, 6], F32, name="stats")
+        for g in range(G):
+            nc.vector.bn_stats(out=stats[:, g, :], in_=inp_sb[:, NB * g : NB * (g + 1)])
+        mv = xpool.tile([P, 2], F32, name="mv")
+        nc.vector.bn_aggr(out=mv[:], in_=stats[:].rearrange("n g s -> n (g s)"))
+        ve = xpool.tile([P, 1], F32, name="ve")
+        nc.vector.tensor_scalar_add(ve[:], mv[:, 1:2], LN_EPS)
+        std = xpool.tile([P, 1], F32, name="std")
+        nc.scalar.sqrt(std[:], ve[:])
+        rstd = xpool.tile([P, 1], F32, name="rstd")
+        nc.vector.reciprocal(rstd[:], std[:])
+        nmr = xpool.tile([P, 1], F32, name="nmr")
+        nc.vector.scalar_tensor_tensor(
+            out=nmr[:], in0=mv[:, 0:1], scalar=-1.0, in1=rstd[:], op0=ALU.mult, op1=ALU.mult
+        )
+
+        xc = xpool.tile([P, G, P], U32, name="xc", align_bytes=64)
+        xs = xpool.tile([P, G, P], U8, name="xs", align_bytes=64)
+        for g in range(G):
+            xh = xpool.tile([P, 4, P], F32, name="xh", tag="xh", bufs=3)
+            nc.scalar.activation(
+                out=xh[:],
+                in_=inp_sb[:, NB * g : NB * (g + 1)].rearrange("n (p t) -> n t p", t=4),
+                func=ACT.Identity,
+                scale=rstd[:, 0:1],
+                bias=nmr[:, 0:1],
+            )
+            xt = auxp.tile([P, 4, P], F32, name="xt", tag="aux")
+            for t in range(4):
+                nc.tensor.transpose(xt[:, t, :], xh[:, t, :], ident_f[:])
+            grouped = xpool.tile([P, P, 4], BF16, name="grouped", tag="grouped", bufs=3, align_bytes=64)
+            for t in range(4):
+                nc.vector.tensor_scalar(
+                    out=grouped[:, :, t],
+                    in0=xt[:, t, :],
+                    scalar1=gb[:, g, t : t + 1],
+                    scalar2=gb[:, 5 + g, t : t + 1],
+                    op0=ALU.mult,
+                    op1=ALU.add,
+                )
+            nc.vector.quantize_mx(
+                out=xc[:, g, :].bitcast(FP8X4),
+                scales=xs[:, g, :],
+                in_=grouped[:].rearrange("p n t -> p (n t)"),
+            )
+
+        q_dram = out_0[0].rearrange("h n j -> n h j")
+        v_dram = out_2[0].rearrange("h n j -> n h j")
+        k_dram = out_1.rearrange("o h j n -> (o h j n)").rearrange("(H p f) -> p H f", p=P, f=NB)
+
+        def k_block(H):
+            kt = auxp.tile([P, 4, P], F32, name="kt", tag="aux")
+            for e in range(4):
+                nc.tensor.transpose(kt[:, e, :], ks[:, H, e, :], ident_f[:])
+            nc.scalar.copy(out=k2[:, H, :], in_=kt[:].rearrange("p e n -> p (e n)"))
+            nc.sync.dma_start(out=k_dram[:, H, :], in_=k2[:, H, :])
+
+        for r in range(3):
+            for b in range(BANKS):
+                bias_chunk(BANKS * r + b)
+            accs = [accp.tile([P, NB], F32, name="acc%d" % b, tag="acc") for b in range(BANKS)]
+            for g in range(G):
+                k0 = 4 * g if g < 4 else 4 * r
+                c0 = RW * r if g < 4 else 3 * RW
+                for b in range(BANKS):
+                    nc.tensor.matmul_mx(
+                        out=accs[b][:],
+                        lhsT=xc[:, g, :].bitcast(FP8X4),
+                        lhsT_scale=xs[:, g, :],
+                        rhs=words[r][g][:, NB * b : NB * (b + 1)].bitcast(FP8X4),
+                        rhs_scale=planes[k0:P, c0 + NB * b : c0 + NB * (b + 1)],
+                        start=(g == 0),
+                        stop=(g == G - 1),
+                    )
+            for b in range(BANKS):
+                acc = accs[b]
+                if r < 2:
+                    B = BANKS * r + b
+                    q_sl = q_sb[:, 256 * B : 256 * (B + 1)]
+                    nc.vector.tensor_tensor(
+                        out=q_sl, in0=acc[:].rearrange("n (i two) -> n two i", two=2)[:, 0, :], in1=q_sl, op=ALU.add
+                    )
+                    k_sl = ks[:, B // 2, :, 64 * (B % 2) : 64 * (B % 2) + 64]
+                    nc.vector.tensor_tensor(
+                        out=k_sl,
+                        in0=acc[:].rearrange("n (pp e two) -> n two e pp", e=4, two=2)[:, 1],
+                        in1=k_sl,
+                        op=ALU.add,
+                    )
+                    if B % 2 == 1:
+                        k_block(B // 2)
+                else:
+                    v_sl = v_sb[:, NB * b : NB * (b + 1)]
+                    nc.vector.tensor_tensor(out=v_sl, in0=acc[:], in1=v_sl, op=ALU.add)
+                    nc.sync.dma_start(
+                        out=v_dram[:, 4 * b : 4 * (b + 1), :], in_=v_sl.rearrange("n (h j) -> n h j", j=P)
+                    )
+            if r < 2:
+                nc.sync.dma_start(
+                    out=q_dram[:, 10 * r : 10 * (r + 1), :],
+                    in_=q_sb[:, 1280 * r : 1280 * (r + 1)].rearrange("n (h j) -> n h j", j=P),
+                )

@@ -20,7 +20,6 @@ RW = 2560
 BANKS = RW // NB
 LN_EPS = 1e-5
 FLOPS = 2 * 128 * 2560 * 7680
-SCALES_ON_GPSIMD = False
 
 
 def tile_relational_w_kernel(
@@ -34,9 +33,11 @@ def tile_relational_w_kernel(
         opool = ctx.enter_context(tc.tile_pool(name="opool", bufs=1))
         accp = ctx.enter_context(tc.psum_pool(name="accp", bufs=6))
         auxp = ctx.enter_context(tc.psum_pool(name="auxp", bufs=2))
+        ctx.enter_context(tc.manual_schedule(engines={mybir.EngineType.SP}))
 
         planes = wpool.tile([P, 4 * RW], U8, name="planes", align_bytes=64)
         rows = const.tile([P, NB], BF16, name="rows")
+        grows = const.tile([P, NB], BF16, name="grows")
         warm = const.tile([P, 1], F32, name="warm")
         ident_f = const.tile([P, P], F32, name="ident_f")
         ident_b = const.tile([P, P], BF16, name="ident_b")
@@ -47,25 +48,30 @@ def tile_relational_w_kernel(
         ks = opool.tile([P, G, 4, P], F32, name="ks")
         k2 = opool.tile([P, G, NB], F32, name="k2")
 
-        nc.vector.memset(planes[:].bitcast(I32), 0)
+        nc.vector.memset(grows[:], 0.0)
         nc.vector.memset(rows[:], 0.0)
-        nc.vector.memset(warm[:], 1.0)
+        nc.vector.memset(planes[:].bitcast(I32), 0)
+        nc.scalar.dma_start(out=grows[0:5, :], in_=gamma.rearrange("(r c) -> r c", c=NB))
+        nc.scalar.dma_start(out=grows[5:10, :], in_=beta.rearrange("(r c) -> r c", c=NB))
+        nc.scalar.dma_start(out=rows[0:10, :], in_=b_qk.rearrange("(r c) -> r c", c=NB))
+        nc.scalar.dma_start(out=rows[10:15, :], in_=b_v.rearrange("(r c) -> r c", c=NB))
+        nc.gpsimd.memset(warm[:], 1.0)
         nc.scalar.sqrt(warm[:], warm[:])
         make_identity(nc, ident_b[:])
         make_identity(nc, ident_f[:])
 
-        nc.sync.dma_start(out=inp_sb[:], in_=inp[0])
-        nc.scalar.dma_start(out=rows[15:20, :], in_=gamma.rearrange("(r c) -> r c", c=NB))
-        nc.scalar.dma_start(out=rows[20:25, :], in_=beta.rearrange("(r c) -> r c", c=NB))
-        nc.scalar.dma_start(out=rows[0:10, :], in_=b_qk.rearrange("(r c) -> r c", c=NB))
-        nc.scalar.dma_start(out=rows[10:15, :], in_=b_v.rearrange("(r c) -> r c", c=NB))
+        def word_dma(r, g):
+            if r < 2:
+                src = W_qk_words[g].rearrange("p n t -> p (n t)")[:, 4 * RW * r : 4 * RW * (r + 1)]
+            else:
+                src = W_v_words[g].rearrange("p n t -> p (n t)")
+            nc.sync.dma_start(out=words[r][g][:], in_=src.bitcast(I32))
 
         def scale_dma(dst, src):
-            if SCALES_ON_GPSIMD:
-                nc.gpsimd.dma_start(out=dst.bitcast(F32), in_=src.bitcast(F32))
-            else:
-                nc.sync.dma_start(out=dst.bitcast(I32), in_=src.bitcast(I32))
+            nc.sync.dma_start(out=dst.bitcast(I32), in_=src.bitcast(I32))
 
+        nc.sync.dma_start(out=inp_sb[:], in_=inp[0])
+        word_dma(0, 0)
         for Q in range(4):
             scale_dma(planes[32 * Q : 32 * Q + 16, 0 : 2 * RW], W_qk_scales[0:4, 4 * Q : 4 * Q + 4, :])
         for Q in range(4):
@@ -77,22 +83,16 @@ def tile_relational_w_kernel(
             scale_dma(planes[32 * Q : 32 * Q + 16, 2 * RW : 3 * RW], W_v_scales[0:4, 4 * Q : 4 * Q + 4, :])
         for Q in range(4):
             scale_dma(planes[32 * Q + 8 : 32 * Q + 12, 3 * RW : 4 * RW], W_v_scales[4, 4 * Q : 4 * Q + 4, :])
-
-        for r in range(3):
-            for g in range(G):
-                if r < 2:
-                    src = W_qk_words[g].rearrange("p n t -> p (n t)")[:, 4 * RW * r : 4 * RW * (r + 1)]
-                else:
-                    src = W_v_words[g].rearrange("p n t -> p (n t)")
-                nc.sync.dma_start(out=words[r][g][:], in_=src.bitcast(I32))
+        for i in range(1, 3 * G):
+            word_dma(i // G, i % G)
 
         rows_s = const.tile([P, 4, P], BF16, name="rows_s")
-        nc.vector.tensor_copy(out=rows_s[:], in_=rows[:].rearrange("r (p t) -> r t p", t=4))
+        nc.vector.tensor_copy(out=rows_s[:], in_=grows[:].rearrange("r (p t) -> r t p", t=4))
         gb_ps = auxp.tile([P, 4, P], BF16, name="gb_ps", tag="aux")
         for t in range(4):
             nc.tensor.transpose(gb_ps[:, t, :], rows_s[:, t, :], ident_b[:])
         gb = const.tile([P, 10, 4], F32, name="gb")
-        nc.vector.tensor_copy(out=gb[:], in_=gb_ps[:, :, 15:25].rearrange("p t j -> p j t"))
+        nc.vector.tensor_copy(out=gb[:], in_=gb_ps[:, :, 0:10].rearrange("p t j -> p j t"))
 
         def bias_chunk(c):
             pb = auxp.tile([P, NB], F32, name="pb", tag="aux")

@@ -72,14 +72,24 @@ def tile_relational_w_kernel(
 
         nc.sync.dma_start(out=inp_sb[:], in_=inp[0])
         word_dma(0, 0)
-        for Q in range(4):
+        for Q in (2, 3):
+            nc.gpsimd.dma_start(
+                out=planes[32 * Q : 32 * Q + 16, 0 : 2 * RW].bitcast(F32),
+                in_=W_qk_scales[0:4, 4 * Q : 4 * Q + 4, :].bitcast(F32),
+            )
+        for Q in (2, 3):
+            nc.gpsimd.dma_start(
+                out=planes[32 * Q : 32 * Q + 16, 2 * RW : 3 * RW].bitcast(F32),
+                in_=W_v_scales[0:4, 4 * Q : 4 * Q + 4, :].bitcast(F32),
+            )
+        for Q in (0, 1):
             scale_dma(planes[32 * Q : 32 * Q + 16, 0 : 2 * RW], W_qk_scales[0:4, 4 * Q : 4 * Q + 4, :])
         for Q in range(4):
             scale_dma(
                 planes[32 * Q : 32 * Q + 8, 3 * RW : 4 * RW],
                 W_qk_scales[4, 4 * Q : 4 * Q + 4, :].rearrange("r (o c) -> o r c", o=2),
             )
-        for Q in range(4):
+        for Q in (0, 1):
             scale_dma(planes[32 * Q : 32 * Q + 16, 2 * RW : 3 * RW], W_v_scales[0:4, 4 * Q : 4 * Q + 4, :])
         for Q in range(4):
             scale_dma(planes[32 * Q + 8 : 32 * Q + 12, 3 * RW : 4 * RW], W_v_scales[4, 4 * Q : 4 * Q + 4, :])

@@ -72,27 +72,31 @@ def tile_relational_w_kernel(
 
         nc.sync.dma_start(out=inp_sb[:], in_=inp[0])
         word_dma(0, 0)
-        for Q in (2, 3):
-            nc.gpsimd.dma_start(
-                out=planes[32 * Q : 32 * Q + 16, 0 : 2 * RW].bitcast(F32),
-                in_=W_qk_scales[0:4, 4 * Q : 4 * Q + 4, :].bitcast(F32),
-            )
-        for Q in (2, 3):
-            nc.gpsimd.dma_start(
-                out=planes[32 * Q : 32 * Q + 16, 2 * RW : 3 * RW].bitcast(F32),
-                in_=W_v_scales[0:4, 4 * Q : 4 * Q + 4, :].bitcast(F32),
-            )
-        for Q in (0, 1):
-            scale_dma(planes[32 * Q : 32 * Q + 16, 0 : 2 * RW], W_qk_scales[0:4, 4 * Q : 4 * Q + 4, :])
-        for Q in range(4):
-            scale_dma(
+        def plane_qk03(Q):
+            return planes[32 * Q : 32 * Q + 16, 0 : 2 * RW], W_qk_scales[0:4, 4 * Q : 4 * Q + 4, :]
+
+        def plane_qk4(Q):
+            return (
                 planes[32 * Q : 32 * Q + 8, 3 * RW : 4 * RW],
                 W_qk_scales[4, 4 * Q : 4 * Q + 4, :].rearrange("r (o c) -> o r c", o=2),
             )
-        for Q in (0, 1):
-            scale_dma(planes[32 * Q : 32 * Q + 16, 2 * RW : 3 * RW], W_v_scales[0:4, 4 * Q : 4 * Q + 4, :])
-        for Q in range(4):
-            scale_dma(planes[32 * Q + 8 : 32 * Q + 12, 3 * RW : 4 * RW], W_v_scales[4, 4 * Q : 4 * Q + 4, :])
+
+        def plane_v03(Q):
+            return planes[32 * Q : 32 * Q + 16, 2 * RW : 3 * RW], W_v_scales[0:4, 4 * Q : 4 * Q + 4, :]
+
+        def plane_v4(Q):
+            return planes[32 * Q + 8 : 32 * Q + 12, 3 * RW : 4 * RW], W_v_scales[4, 4 * Q : 4 * Q + 4, :]
+
+        for kind, Q in (
+            (plane_v03, 2), (plane_qk03, 2), (plane_qk03, 3), (plane_v03, 3),
+            (plane_v4, 2), (plane_v4, 3), (plane_qk4, 2), (plane_qk4, 3),
+        ):
+            dst, src = kind(Q)
+            nc.gpsimd.dma_start(out=dst.bitcast(F32), in_=src.bitcast(F32))
+        for kind in (plane_qk03, plane_qk4, plane_v03, plane_v4):
+            for Q in (0, 1):
+                dst, src = kind(Q)
+                scale_dma(dst, src)
         for i in range(1, 3 * G):
             word_dma(i // G, i % G)
 

@@ -171,7 +171,7 @@ def tile_relational_w_kernel(
                 in_=grouped[:].rearrange("p n t -> p (n t)"),
             )
 
-        q_dram = out_0[0].rearrange("h n j -> n h j")
+        q_dram = out_0.rearrange("o h n j -> (o h n j)").rearrange("(H p f) -> p H f", p=P, f=NB)
         v_dram = out_2[0].rearrange("h n j -> n h j")
         k_dram = out_1.rearrange("o h j n -> (o h j n)").rearrange("(H p f) -> p H f", p=P, f=NB)
 
@@ -181,6 +181,19 @@ def tile_relational_w_kernel(
                 nc.tensor.transpose(kt[:, e, :], ks[:, H, e, :], ident_f[:])
             nc.scalar.copy(out=k2[:, H, :], in_=kt[:].rearrange("p e n -> p (e n)"))
             nc.sync.dma_start(out=k_dram[:, H, :], in_=k2[:, H, :])
+
+        def q_block(H):
+            q_sl = q_sb[:, NB * H : NB * (H + 1)]
+            q1 = auxp.tile([P, NB], F32, name="q1", tag="aux")
+            for hh in range(4):
+                nc.tensor.transpose(q1[:, P * hh : P * (hh + 1)], q_sl[:, P * hh : P * (hh + 1)], ident_f[:])
+            qt = opool.tile([P, 4, P], F32, name="qt", tag="qt", bufs=2)
+            nc.scalar.copy(out=qt[:], in_=q1[:].rearrange("j (c e) -> j e c", e=4))
+            q2 = auxp.tile([P, 4, P], F32, name="q2", tag="aux")
+            for e in range(4):
+                nc.tensor.transpose(q2[:, e, :], qt[:, e, :], ident_f[:])
+            nc.vector.tensor_copy(out=q_sl, in_=q2[:].rearrange("c e j -> c (e j)"))
+            nc.sync.dma_start(out=q_dram[:, H, :], in_=q_sl)
 
         for r in range(3):
             for b in range(BANKS):
@@ -216,14 +229,10 @@ def tile_relational_w_kernel(
                     )
                     if B % 2 == 1:
                         k_block(B // 2)
+                        q_block(B // 2)
                 else:
                     v_sl = v_sb[:, NB * b : NB * (b + 1)]
                     nc.vector.tensor_tensor(out=v_sl, in0=acc[:], in1=v_sl, op=ALU.add)
                     nc.sync.dma_start(
                         out=v_dram[:, 4 * b : 4 * (b + 1), :], in_=v_sl.rearrange("n (h j) -> n h j", j=P)
                     )
-            if r < 2:
-                nc.sync.dma_start(
-                    out=q_dram[:, 10 * r : 10 * (r + 1), :],
-                    in_=q_sb[:, 1280 * r : 1280 * (r + 1)].rearrange("n (h j) -> n h j", j=P),
-                )

@@ -31,9 +31,18 @@ def tile_relational_w_kernel(
         wpool = ctx.enter_context(tc.tile_pool(name="wpool", bufs=1))
         xpool = ctx.enter_context(tc.tile_pool(name="xpool", bufs=1))
         opool = ctx.enter_context(tc.tile_pool(name="opool", bufs=1))
-        accp = ctx.enter_context(tc.psum_pool(name="accp", bufs=6))
-        auxp = ctx.enter_context(tc.psum_pool(name="auxp", bufs=2))
-        ctx.enter_context(tc.manual_schedule(engines={mybir.EngineType.SP}))
+        accp = ctx.enter_context(tc.psum_pool(name="accp", bufs=1))
+        auxp = ctx.enter_context(tc.psum_pool(name="auxp", bufs=3))
+        ctx.enter_context(
+            tc.manual_schedule(
+                engines={
+                    mybir.EngineType.SP,
+                    mybir.EngineType.PE,
+                    mybir.EngineType.Activation,
+                    mybir.EngineType.DVE,
+                }
+            )
+        )
 
         planes = wpool.tile([P, 4 * RW], U8, name="planes", align_bytes=64)
         rows = const.tile([P, NB], BF16, name="rows")
@@ -70,8 +79,6 @@ def tile_relational_w_kernel(
         def scale_dma(dst, src):
             nc.sync.dma_start(out=dst.bitcast(I32), in_=src.bitcast(I32))
 
-        nc.sync.dma_start(out=inp_sb[:], in_=inp[0])
-        word_dma(0, 0)
         def plane_qk03(Q):
             return planes[32 * Q : 32 * Q + 16, 0 : 2 * RW], W_qk_scales[0:4, 4 * Q : 4 * Q + 4, :]
 
@@ -87,21 +94,34 @@ def tile_relational_w_kernel(
         def plane_v4(Q):
             return planes[32 * Q + 8 : 32 * Q + 12, 3 * RW : 4 * RW], W_v_scales[4, 4 * Q : 4 * Q + 4, :]
 
-        for kind, Q in (
-            (plane_v03, 2), (plane_qk03, 2), (plane_qk03, 3), (plane_v03, 3),
-            (plane_v4, 2), (plane_v4, 3), (plane_qk4, 2), (plane_qk4, 3),
-        ):
-            dst, src = kind(Q)
-            nc.gpsimd.dma_start(out=dst.bitcast(F32), in_=src.bitcast(F32))
+        nc.sync.dma_start(out=inp_sb[:], in_=inp[0])
+        for i in range(1):
+            word_dma(0, i)
         for kind in (plane_qk03, plane_qk4, plane_v03, plane_v4):
-            for Q in (0, 1):
+            for Q in range(4):
                 dst, src = kind(Q)
                 scale_dma(dst, src)
         for i in range(1, 3 * G):
             word_dma(i // G, i % G)
 
+        stats = xpool.tile([P, G, 6], F32, name="stats")
+        for g in range(G):
+            nc.vector.bn_stats(out=stats[:, g, :], in_=inp_sb[:, NB * g : NB * (g + 1)])
+        mv = xpool.tile([P, 2], F32, name="mv")
+        nc.vector.bn_aggr(out=mv[:], in_=stats[:].rearrange("n g s -> n (g s)"))
+        ve = xpool.tile([P, 1], F32, name="ve")
+        nc.vector.tensor_scalar_add(ve[:], mv[:, 1:2], LN_EPS)
+        std = xpool.tile([P, 1], F32, name="std")
+        nc.scalar.sqrt(std[:], ve[:])
         rows_s = const.tile([P, 4, P], BF16, name="rows_s")
         nc.vector.tensor_copy(out=rows_s[:], in_=grows[:].rearrange("r (p t) -> r t p", t=4))
+        rstd = xpool.tile([P, 1], F32, name="rstd")
+        nc.vector.reciprocal(rstd[:], std[:])
+        nmr = xpool.tile([P, 1], F32, name="nmr")
+        nc.vector.scalar_tensor_tensor(
+            out=nmr[:], in0=mv[:, 0:1], scalar=-1.0, in1=rstd[:], op0=ALU.mult, op1=ALU.mult
+        )
+
         gb_ps = auxp.tile([P, 4, P], BF16, name="gb_ps", tag="aux")
         for t in range(4):
             nc.tensor.transpose(gb_ps[:, t, :], rows_s[:, t, :], ident_b[:])
@@ -125,25 +145,10 @@ def tile_relational_w_kernel(
             else:
                 nc.scalar.copy(out=v_sb[:, NB * (c - 10) : NB * (c - 9)], in_=pb[:])
 
-        stats = xpool.tile([P, G, 6], F32, name="stats")
-        for g in range(G):
-            nc.vector.bn_stats(out=stats[:, g, :], in_=inp_sb[:, NB * g : NB * (g + 1)])
-        mv = xpool.tile([P, 2], F32, name="mv")
-        nc.vector.bn_aggr(out=mv[:], in_=stats[:].rearrange("n g s -> n (g s)"))
-        ve = xpool.tile([P, 1], F32, name="ve")
-        nc.vector.tensor_scalar_add(ve[:], mv[:, 1:2], LN_EPS)
-        std = xpool.tile([P, 1], F32, name="std")
-        nc.scalar.sqrt(std[:], ve[:])
-        rstd = xpool.tile([P, 1], F32, name="rstd")
-        nc.vector.reciprocal(rstd[:], std[:])
-        nmr = xpool.tile([P, 1], F32, name="nmr")
-        nc.vector.scalar_tensor_tensor(
-            out=nmr[:], in0=mv[:, 0:1], scalar=-1.0, in1=rstd[:], op0=ALU.mult, op1=ALU.mult
-        )
-
         xc = xpool.tile([P, G, P], U32, name="xc", align_bytes=64)
         xs = xpool.tile([P, G, P], U8, name="xs", align_bytes=64)
-        for g in range(G):
+
+        def x_rows(g):
             xh = xpool.tile([P, 4, P], F32, name="xh", tag="xh", bufs=3)
             nc.scalar.activation(
                 out=xh[:],
@@ -165,40 +170,75 @@ def tile_relational_w_kernel(
                     op0=ALU.mult,
                     op1=ALU.add,
                 )
+            return grouped
+
+        def x_quantise(g, grouped):
             nc.vector.quantize_mx(
                 out=xc[:, g, :].bitcast(FP8X4),
                 scales=xs[:, g, :],
                 in_=grouped[:].rearrange("p n t -> p (n t)"),
             )
 
-        q_dram = out_0.rearrange("o h n j -> (o h n j)").rearrange("(H p f) -> p H f", p=P, f=NB)
-        v_dram = out_2[0].rearrange("h n j -> n h j")
-        k_dram = out_1.rearrange("o h j n -> (o h j n)").rearrange("(H p f) -> p H f", p=P, f=NB)
+        grouped = x_rows(0)
+        for g in range(1, G):
+            ahead = x_rows(g)
+            x_quantise(g - 1, grouped)
+            grouped = ahead
+        x_quantise(G - 1, grouped)
 
-        def k_block(H):
+        for c in range(BANKS):
+            bias_chunk(c)
+
+        q_dram = out_0.rearrange("o h n j -> (o h n j)").rearrange("(H p f) -> p H f", p=P, f=NB)
+        k_dram = out_1.rearrange("o h j n -> (o h j n)").rearrange("(H p f) -> p H f", p=P, f=NB)
+        v_dram = out_2[0].rearrange("h n j -> n h j")
+
+        def k_turn(H):
             kt = auxp.tile([P, 4, P], F32, name="kt", tag="aux")
             for e in range(4):
                 nc.tensor.transpose(kt[:, e, :], ks[:, H, e, :], ident_f[:])
             nc.scalar.copy(out=k2[:, H, :], in_=kt[:].rearrange("p e n -> p (e n)"))
             nc.sync.dma_start(out=k_dram[:, H, :], in_=k2[:, H, :])
 
-        def q_block(H):
-            q_sl = q_sb[:, NB * H : NB * (H + 1)]
+        turned = {}
+
+        def q_turn(H):
             q1 = auxp.tile([P, NB], F32, name="q1", tag="aux")
             for hh in range(4):
-                nc.tensor.transpose(q1[:, P * hh : P * (hh + 1)], q_sl[:, P * hh : P * (hh + 1)], ident_f[:])
+                col = NB * H + P * hh
+                nc.tensor.transpose(q1[:, P * hh : P * (hh + 1)], q_sb[:, col : col + P], ident_f[:])
             qt = opool.tile([P, 4, P], F32, name="qt", tag="qt", bufs=2)
             nc.scalar.copy(out=qt[:], in_=q1[:].rearrange("j (c e) -> j e c", e=4))
+            turned[H] = qt
+
+        def q_back(H):
             q2 = auxp.tile([P, 4, P], F32, name="q2", tag="aux")
             for e in range(4):
-                nc.tensor.transpose(q2[:, e, :], qt[:, e, :], ident_f[:])
+                nc.tensor.transpose(q2[:, e, :], turned[H][:, e, :], ident_f[:])
+            q_sl = q_sb[:, NB * H : NB * (H + 1)]
             nc.vector.tensor_copy(out=q_sl, in_=q2[:].rearrange("c e j -> c (e j)"))
             nc.sync.dma_start(out=q_dram[:, H, :], in_=q_sl)
 
+        after = {
+            0: [[(bias_chunk, BANKS + g), (bias_chunk, 2 * BANKS + g)] for g in range(G)],
+            1: [
+                [(k_turn, 0), (q_turn, 0)],
+                [(q_back, 0), (k_turn, 1)],
+                [(q_turn, 1)],
+                [(q_back, 1)],
+                [],
+            ],
+            2: [
+                [(k_turn, 2), (q_turn, 2), (k_turn, 3)],
+                [(q_back, 2), (q_turn, 3), (k_turn, 4)],
+                [(q_back, 3), (q_turn, 4)],
+                [(q_back, 4)],
+                [],
+            ],
+        }
+
         for r in range(3):
-            for b in range(BANKS):
-                bias_chunk(BANKS * r + b)
-            accs = [accp.tile([P, NB], F32, name="acc%d" % b, tag="acc") for b in range(BANKS)]
+            accs = [accp.tile([P, NB], F32, name="acc%d" % b, tag="acc%d" % b) for b in range(BANKS)]
             for g in range(G):
                 k0 = 4 * g if g < 4 else 4 * r
                 c0 = RW * r if g < 4 else 3 * RW
@@ -212,6 +252,8 @@ def tile_relational_w_kernel(
                         start=(g == 0),
                         stop=(g == G - 1),
                     )
+                for step, arg in after[r][g]:
+                    step(arg)
             for b in range(BANKS):
                 acc = accs[b]
                 if r < 2:
@@ -227,9 +269,6 @@ def tile_relational_w_kernel(
                         in1=k_sl,
                         op=ALU.add,
                     )
-                    if B % 2 == 1:
-                        k_block(B // 2)
-                        q_block(B // 2)
                 else:
                     v_sl = v_sb[:, NB * b : NB * (b + 1)]
                     nc.vector.tensor_tensor(out=v_sl, in0=acc[:], in1=v_sl, op=ALU.add)

@@ -98,7 +98,10 @@ def tile_relational_w_kernel(
         for i in range(1):
             word_dma(0, i)
         for kind in (plane_qk03, plane_qk4, plane_v03, plane_v4):
-            for Q in range(4):
+            for Q in (2, 3):
+                dst, src = kind(Q)
+                nc.gpsimd.dma_start(out=dst.bitcast(F32), in_=src.bitcast(F32))
+            for Q in (0, 1):
                 dst, src = kind(Q)
                 scale_dma(dst, src)
         for i in range(1, 3 * G):
@@ -189,7 +192,7 @@ def tile_relational_w_kernel(
         for c in range(BANKS):
             bias_chunk(c)
 
-        q_dram = out_0.rearrange("o h n j -> (o h n j)").rearrange("(H p f) -> p H f", p=P, f=NB)
+        q_dram = out_0[0].rearrange("h n j -> n h j")
         k_dram = out_1.rearrange("o h j n -> (o h j n)").rearrange("(H p f) -> p H f", p=P, f=NB)
         v_dram = out_2[0].rearrange("h n j -> n h j")
 
@@ -200,41 +203,10 @@ def tile_relational_w_kernel(
             nc.scalar.copy(out=k2[:, H, :], in_=kt[:].rearrange("p e n -> p (e n)"))
             nc.sync.dma_start(out=k_dram[:, H, :], in_=k2[:, H, :])
 
-        turned = {}
-
-        def q_turn(H):
-            q1 = auxp.tile([P, NB], F32, name="q1", tag="aux")
-            for hh in range(4):
-                col = NB * H + P * hh
-                nc.tensor.transpose(q1[:, P * hh : P * (hh + 1)], q_sb[:, col : col + P], ident_f[:])
-            qt = opool.tile([P, 4, P], F32, name="qt", tag="qt", bufs=2)
-            nc.scalar.copy(out=qt[:], in_=q1[:].rearrange("j (c e) -> j e c", e=4))
-            turned[H] = qt
-
-        def q_back(H):
-            q2 = auxp.tile([P, 4, P], F32, name="q2", tag="aux")
-            for e in range(4):
-                nc.tensor.transpose(q2[:, e, :], turned[H][:, e, :], ident_f[:])
-            q_sl = q_sb[:, NB * H : NB * (H + 1)]
-            nc.vector.tensor_copy(out=q_sl, in_=q2[:].rearrange("c e j -> c (e j)"))
-            nc.sync.dma_start(out=q_dram[:, H, :], in_=q_sl)
-
         after = {
             0: [[(bias_chunk, BANKS + g), (bias_chunk, 2 * BANKS + g)] for g in range(G)],
-            1: [
-                [(k_turn, 0), (q_turn, 0)],
-                [(q_back, 0), (k_turn, 1)],
-                [(q_turn, 1)],
-                [(q_back, 1)],
-                [],
-            ],
-            2: [
-                [(k_turn, 2), (q_turn, 2), (k_turn, 3)],
-                [(q_back, 2), (q_turn, 3), (k_turn, 4)],
-                [(q_back, 3), (q_turn, 4)],
-                [(q_back, 4)],
-                [],
-            ],
+            1: [[(k_turn, 0)], [(k_turn, 1)], [], [], []],
+            2: [[(k_turn, 2)], [(k_turn, 3)], [(k_turn, 4)], [], []],
         }
 
         for r in range(3):
@@ -254,6 +226,11 @@ def tile_relational_w_kernel(
                     )
                 for step, arg in after[r][g]:
                     step(arg)
+                if r > 0 and g == 2:
+                    nc.sync.dma_start(
+                        out=q_dram[:, 10 * (r - 1) : 10 * r, :],
+                        in_=q_sb[:, 1280 * (r - 1) : 1280 * r].rearrange("n (h j) -> n h j", j=P),
+                    )
             for b in range(BANKS):
                 acc = accs[b]
                 if r < 2:

@@ -97,11 +97,12 @@ def tile_relational_w_kernel(
         nc.sync.dma_start(out=inp_sb[:], in_=inp[0])
         for i in range(1):
             word_dma(0, i)
-        for kind in (plane_qk03, plane_qk4, plane_v03, plane_v4):
-            for Q in (2, 3):
+        for kind in (plane_qk4, plane_v03):
+            for Q in range(4):
                 dst, src = kind(Q)
                 nc.gpsimd.dma_start(out=dst.bitcast(F32), in_=src.bitcast(F32))
-            for Q in (0, 1):
+        for kind in (plane_qk03, plane_v4):
+            for Q in range(4):
                 dst, src = kind(Q)
                 scale_dma(dst, src)
         for i in range(1, 3 * G):
@@ -189,7 +190,7 @@ def tile_relational_w_kernel(
             grouped = ahead
         x_quantise(G - 1, grouped)
 
-        for c in range(BANKS):
+        for c in range(3 * BANKS):
             bias_chunk(c)
 
         q_dram = out_0[0].rearrange("h n j -> n h j")
@@ -203,11 +204,7 @@ def tile_relational_w_kernel(
             nc.scalar.copy(out=k2[:, H, :], in_=kt[:].rearrange("p e n -> p (e n)"))
             nc.sync.dma_start(out=k_dram[:, H, :], in_=k2[:, H, :])
 
-        after = {
-            0: [[(bias_chunk, BANKS + g), (bias_chunk, 2 * BANKS + g)] for g in range(G)],
-            1: [[(k_turn, 0)], [(k_turn, 1)], [], [], []],
-            2: [[(k_turn, 2)], [(k_turn, 3)], [(k_turn, 4)], [], []],
-        }
+        after = {(1, 0): 0, (1, 1): 1, (2, 0): 2, (2, 1): 3, (2, 2): 4}
 
         for r in range(3):
             accs = [accp.tile([P, NB], F32, name="acc%d" % b, tag="acc%d" % b) for b in range(BANKS)]
@@ -224,8 +221,8 @@ def tile_relational_w_kernel(
                         start=(g == 0),
                         stop=(g == G - 1),
                     )
-                for step, arg in after[r][g]:
-                    step(arg)
+                if (r, g) in after:
+                    k_turn(after[r, g])
                 if r > 0 and g == 2:
                     nc.sync.dma_start(
                         out=q_dram[:, 10 * (r - 1) : 10 * r, :],

@@ -44,18 +44,18 @@ def tile_relational_w_kernel(
             )
         )
 
-        planes = wpool.tile([P, 4 * RW], U8, name="planes", align_bytes=64)
+        planes = wpool.tile([P, 4 * RW], U8, name="planes", align_bytes=256)
         rows = const.tile([P, NB], BF16, name="rows")
         grows = const.tile([P, NB], BF16, name="grows")
         warm = const.tile([P, 1], F32, name="warm")
         ident_f = const.tile([P, P], F32, name="ident_f")
         ident_b = const.tile([P, P], BF16, name="ident_b")
-        inp_sb = xpool.tile([P, D], BF16, name="inp_sb")
-        words = [[wpool.tile([P, RW], I32, name="w%d_%d" % (r, g), align_bytes=64) for g in range(G)] for r in range(3)]
-        q_sb = opool.tile([P, D], F32, name="q_sb")
-        v_sb = opool.tile([P, D], F32, name="v_sb")
+        inp_sb = xpool.tile([P, D], BF16, name="inp_sb", align_bytes=256)
+        words = [[wpool.tile([P, RW], I32, name="w%d_%d" % (r, g), align_bytes=256) for g in range(G)] for r in range(3)]
+        q_sb = opool.tile([P, D], F32, name="q_sb", align_bytes=256)
+        v_sb = opool.tile([P, D], F32, name="v_sb", align_bytes=256)
         ks = opool.tile([P, G, 4, P], F32, name="ks")
-        k2 = opool.tile([P, G, NB], F32, name="k2")
+        k2 = opool.tile([P, G, NB], F32, name="k2", align_bytes=256)
 
         nc.vector.memset(grows[:], 0.0)
         nc.vector.memset(rows[:], 0.0)

@@ -45,6 +45,7 @@ def tile_relational_w_kernel(
         )
 
         planes = wpool.tile([P, 4 * RW], U8, name="planes", align_bytes=256)
+        planes_v4 = wpool.tile([P, RW], U8, name="planes_v4", align_bytes=256)
         rows = const.tile([P, NB], BF16, name="rows")
         grows = const.tile([P, NB], BF16, name="grows")
         warm = const.tile([P, 1], F32, name="warm")
@@ -60,6 +61,7 @@ def tile_relational_w_kernel(
         nc.vector.memset(grows[:], 0.0)
         nc.vector.memset(rows[:], 0.0)
         nc.vector.memset(planes[:].bitcast(I32), 0)
+        nc.vector.memset(planes_v4[:].bitcast(I32), 0)
         nc.scalar.dma_start(out=grows[0:5, :], in_=gamma.rearrange("(r c) -> r c", c=NB))
         nc.scalar.dma_start(out=grows[5:10, :], in_=beta.rearrange("(r c) -> r c", c=NB))
         nc.scalar.dma_start(out=rows[0:10, :], in_=b_qk.rearrange("(r c) -> r c", c=NB))
@@ -76,9 +78,6 @@ def tile_relational_w_kernel(
                 src = W_v_words[g].rearrange("p n t -> p (n t)")
             nc.sync.dma_start(out=words[r][g][:], in_=src.bitcast(I32))
 
-        def scale_dma(dst, src):
-            nc.sync.dma_start(out=dst.bitcast(I32), in_=src.bitcast(I32))
-
         def plane_qk03(Q):
             return planes[32 * Q : 32 * Q + 16, 0 : 2 * RW], W_qk_scales[0:4, 4 * Q : 4 * Q + 4, :]
 
@@ -92,21 +91,15 @@ def tile_relational_w_kernel(
             return planes[32 * Q : 32 * Q + 16, 2 * RW : 3 * RW], W_v_scales[0:4, 4 * Q : 4 * Q + 4, :]
 
         def plane_v4(Q):
-            return planes[32 * Q + 8 : 32 * Q + 12, 3 * RW : 4 * RW], W_v_scales[4, 4 * Q : 4 * Q + 4, :]
+            return planes_v4[32 * Q : 32 * Q + 4, :], W_v_scales[4, 4 * Q : 4 * Q + 4, :]
 
         nc.sync.dma_start(out=inp_sb[:], in_=inp[0])
-        for i in range(1):
-            word_dma(0, i)
-        for kind in (plane_qk4, plane_v03):
+        for i in range(3 * G):
+            word_dma(i // G, i % G)
+        for kind in (plane_qk03, plane_qk4, plane_v03, plane_v4):
             for Q in range(4):
                 dst, src = kind(Q)
                 nc.gpsimd.dma_start(out=dst.bitcast(F32), in_=src.bitcast(F32))
-        for kind in (plane_qk03, plane_v4):
-            for Q in range(4):
-                dst, src = kind(Q)
-                scale_dma(dst, src)
-        for i in range(1, 3 * G):
-            word_dma(i // G, i % G)
 
         stats = xpool.tile([P, G, 6], F32, name="stats")
         for g in range(G):
@@ -209,15 +202,19 @@ def tile_relational_w_kernel(
         for r in range(3):
             accs = [accp.tile([P, NB], F32, name="acc%d" % b, tag="acc%d" % b) for b in range(BANKS)]
             for g in range(G):
-                k0 = 4 * g if g < 4 else 4 * r
-                c0 = RW * r if g < 4 else 3 * RW
+                if g < 4:
+                    plane = planes[4 * g : P, RW * r : RW * (r + 1)]
+                elif r < 2:
+                    plane = planes[4 * r : P, 3 * RW : 4 * RW]
+                else:
+                    plane = planes_v4[:]
                 for b in range(BANKS):
                     nc.tensor.matmul_mx(
                         out=accs[b][:],
                         lhsT=xc[:, g, :].bitcast(FP8X4),
                         lhsT_scale=xs[:, g, :],
                         rhs=words[r][g][:, NB * b : NB * (b + 1)].bitcast(FP8X4),
-                        rhs_scale=planes[k0:P, c0 + NB * b : c0 + NB * (b + 1)],
+                        rhs_scale=plane[:, NB * b : NB * (b + 1)],
                         start=(g == 0),
                         stop=(g == G - 1),
                     )

@@ -72,11 +72,19 @@ def tile_relational_w_kernel(
         make_identity(nc, ident_f[:])
 
         def word_dma(r, g):
+            if (r, g) == (2, G - 1):
+                src = W_v_words[g].rearrange("p n t -> p (n t)")
+                for lo, hi in ((0, 3 * NB), (3 * NB, RW)):
+                    nc.sync.dma_start(out=words[r][g][:, lo:hi], in_=src[:, 4 * lo : 4 * hi].bitcast(I32))
+                return
             if r < 2:
                 src = W_qk_words[g].rearrange("p n t -> p (n t)")[:, 4 * RW * r : 4 * RW * (r + 1)]
             else:
                 src = W_v_words[g].rearrange("p n t -> p (n t)")
             nc.sync.dma_start(out=words[r][g][:], in_=src.bitcast(I32))
+
+        def scale_dma(dst, src):
+            nc.sync.dma_start(out=dst.bitcast(I32), in_=src.bitcast(I32))
 
         def plane_qk03(Q):
             return planes[32 * Q : 32 * Q + 16, 0 : 2 * RW], W_qk_scales[0:4, 4 * Q : 4 * Q + 4, :]
@@ -94,12 +102,17 @@ def tile_relational_w_kernel(
             return planes_v4[32 * Q : 32 * Q + 4, :], W_v_scales[4, 4 * Q : 4 * Q + 4, :]
 
         nc.sync.dma_start(out=inp_sb[:], in_=inp[0])
-        for i in range(3 * G):
-            word_dma(i // G, i % G)
+        for i in range(1):
+            word_dma(0, i)
         for kind in (plane_qk03, plane_qk4, plane_v03, plane_v4):
-            for Q in range(4):
+            for Q in (2, 3):
                 dst, src = kind(Q)
                 nc.gpsimd.dma_start(out=dst.bitcast(F32), in_=src.bitcast(F32))
+            for Q in (0, 1):
+                dst, src = kind(Q)
+                scale_dma(dst, src)
+        for i in range(1, 3 * G):
+            word_dma(i // G, i % G)
 
         stats = xpool.tile([P, G, 6], F32, name="stats")
         for g in range(G):
@@ -142,8 +155,8 @@ def tile_relational_w_kernel(
             else:
                 nc.scalar.copy(out=v_sb[:, NB * (c - 10) : NB * (c - 9)], in_=pb[:])
 
-        xc = xpool.tile([P, G, P], U32, name="xc", align_bytes=64)
-        xs = xpool.tile([P, G, P], U8, name="xs", align_bytes=64)
+        xc = xpool.tile([P, G, P], U32, name="xc", align_bytes=256)
+        xs = xpool.tile([P, G, 2 * P], U8, name="xs", align_bytes=256)
 
         def x_rows(g):
             xh = xpool.tile([P, 4, P], F32, name="xh", tag="xh", bufs=3)
@@ -172,7 +185,7 @@ def tile_relational_w_kernel(
         def x_quantise(g, grouped):
             nc.vector.quantize_mx(
                 out=xc[:, g, :].bitcast(FP8X4),
-                scales=xs[:, g, :],
+                scales=xs[:, g, 0:P],
                 in_=grouped[:].rearrange("p n t -> p (n t)"),
             )
 
@@ -212,7 +225,7 @@ def tile_relational_w_kernel(
                     nc.tensor.matmul_mx(
                         out=accs[b][:],
                         lhsT=xc[:, g, :].bitcast(FP8X4),
-                        lhsT_scale=xs[:, g, :],
+                        lhsT_scale=xs[:, g, 0:P],
                         rhs=words[r][g][:, NB * b : NB * (b + 1)].bitcast(FP8X4),
                         rhs_scale=plane[:, NB * b : NB * (b + 1)],
                         start=(g == 0),

from contextlib import ExitStack

import concourse.mybir as mybir
from concourse.masks import make_identity

F32 = mybir.dt.float32
BF16 = mybir.dt.bfloat16
I32 = mybir.dt.int32
U32 = mybir.dt.uint32
U8 = mybir.dt.uint8
FP8X4 = mybir.dt.float8_e4m3fn_x4
ALU = mybir.AluOpType
ACT = mybir.ActivationFunctionType

P = 128
D = 2560
G = 5
NB = 512
RW = 2560
BANKS = RW // NB
LN_EPS = 1e-5
FLOPS = 2 * 128 * 2560 * 7680


def tile_relational_w_kernel(
    tc, inp, gamma, beta, W_qk_words, W_qk_scales, b_qk, W_v_words, W_v_scales, b_v, out_0, out_1, out_2
):
    nc = tc.nc
    with ExitStack() as ctx:
        const = ctx.enter_context(tc.tile_pool(name="const", bufs=1))
        wpool = ctx.enter_context(tc.tile_pool(name="wpool", bufs=1))
        xpool = ctx.enter_context(tc.tile_pool(name="xpool", bufs=1))
        opool = ctx.enter_context(tc.tile_pool(name="opool", bufs=1))
        accp = ctx.enter_context(tc.psum_pool(name="accp", bufs=1))
        auxp = ctx.enter_context(tc.psum_pool(name="auxp", bufs=3))
        ctx.enter_context(
            tc.manual_schedule(
                engines={
                    mybir.EngineType.SP,
                    mybir.EngineType.PE,
                    mybir.EngineType.Activation,
                    mybir.EngineType.DVE,
                }
            )
        )

        planes = wpool.tile([P, 4 * RW], U8, name="planes", align_bytes=256)
        planes_v4 = wpool.tile([P, RW], U8, name="planes_v4", align_bytes=256)
        rows = const.tile([P, NB], BF16, name="rows")
        grows = const.tile([P, NB], BF16, name="grows")
        warm = const.tile([P, 1], F32, name="warm")
        ident_f = const.tile([P, P], F32, name="ident_f")
        ident_b = const.tile([P, P], BF16, name="ident_b")
        inp_sb = xpool.tile([P, D], BF16, name="inp_sb", align_bytes=256)
        words = [[wpool.tile([P, RW], I32, name="w%d_%d" % (r, g), align_bytes=256) for g in range(G)] for r in range(3)]
        q_sb = opool.tile([P, D], F32, name="q_sb", align_bytes=256)
        v_sb = opool.tile([P, D], F32, name="v_sb", align_bytes=256)
        ks = opool.tile([P, G, 4, P], F32, name="ks")
        k2 = opool.tile([P, G, NB], F32, name="k2", align_bytes=256)

        nc.vector.memset(grows[:], 0.0)
        nc.vector.memset(rows[:], 0.0)
        nc.vector.memset(planes[:].bitcast(I32), 0)
        nc.vector.memset(planes_v4[:].bitcast(I32), 0)
        nc.scalar.dma_start(out=grows[0:5, :], in_=gamma.rearrange("(r c) -> r c", c=NB))
        nc.scalar.dma_start(out=grows[5:10, :], in_=beta.rearrange("(r c) -> r c", c=NB))
        nc.scalar.dma_start(out=rows[0:10, :], in_=b_qk.rearrange("(r c) -> r c", c=NB))
        nc.scalar.dma_start(out=rows[10:15, :], in_=b_v.rearrange("(r c) -> r c", c=NB))
        nc.gpsimd.memset(warm[:], 1.0)
        nc.scalar.sqrt(warm[:], warm[:])
        make_identity(nc, ident_b[:])
        make_identity(nc, ident_f[:])

        def word_dma(r, g):
            if (r, g) == (2, G - 1):
                src = W_v_words[g].rearrange("p n t -> p (n t)")
                for lo, hi in ((0, 3 * NB), (3 * NB, RW)):
                    nc.sync.dma_start(out=words[r][g][:, lo:hi], in_=src[:, 4 * lo : 4 * hi].bitcast(I32))
                return
            if r < 2:
                src = W_qk_words[g].rearrange("p n t -> p (n t)")[:, 4 * RW * r : 4 * RW * (r + 1)]
            else:
                src = W_v_words[g].rearrange("p n t -> p (n t)")
            nc.sync.dma_start(out=words[r][g][:], in_=src.bitcast(I32))

        def scale_dma(dst, src):
            nc.sync.dma_start(out=dst.bitcast(I32), in_=src.bitcast(I32))

        def plane_qk03(Q):
            return planes[32 * Q : 32 * Q + 16, 0 : 2 * RW], W_qk_scales[0:4, 4 * Q : 4 * Q + 4, :]

        def plane_qk4(Q):
            return (
                planes[32 * Q : 32 * Q + 8, 3 * RW : 4 * RW],
                W_qk_scales[4, 4 * Q : 4 * Q + 4, :].rearrange("r (o c) -> o r c", o=2),
            )

        def plane_v03(Q):
            return planes[32 * Q : 32 * Q + 16, 2 * RW : 3 * RW], W_v_scales[0:4, 4 * Q : 4 * Q + 4, :]

        def plane_v4(Q):
            return planes_v4[32 * Q : 32 * Q + 4, :], W_v_scales[4, 4 * Q : 4 * Q + 4, :]

        nc.sync.dma_start(out=inp_sb[:], in_=inp[0])
        for i in range(1):
            word_dma(0, i)
        for kind in (plane_qk03, plane_qk4, plane_v03, plane_v4):
            for Q in (2, 3):
                dst, src = kind(Q)
                nc.gpsimd.dma_start(out=dst.bitcast(F32), in_=src.bitcast(F32))
            for Q in (0, 1):
                dst, src = kind(Q)
                scale_dma(dst, src)
        for i in range(1, 3 * G):
            word_dma(i // G, i % G)

        stats = xpool.tile([P, G, 6], F32, name="stats")
        for g in range(G):
            nc.vector.bn_stats(out=stats[:, g, :], in_=inp_sb[:, NB * g : NB * (g + 1)])
        mv = xpool.tile([P, 2], F32, name="mv")
        nc.vector.bn_aggr(out=mv[:], in_=stats[:].rearrange("n g s -> n (g s)"))
        ve = xpool.tile([P, 1], F32, name="ve")
        nc.vector.tensor_scalar_add(ve[:], mv[:, 1:2], LN_EPS)
        std = xpool.tile([P, 1], F32, name="std")
        nc.scalar.sqrt(std[:], ve[:])
        rows_s = const.tile([P, 4, P], BF16, name="rows_s")
        nc.vector.tensor_copy(out=rows_s[:], in_=grows[:].rearrange("r (p t) -> r t p", t=4))
        rstd = xpool.tile([P, 1], F32, name="rstd")
        nc.vector.reciprocal(rstd[:], std[:])
        nmr = xpool.tile([P, 1], F32, name="nmr")
        nc.vector.scalar_tensor_tensor(
            out=nmr[:], in0=mv[:, 0:1], scalar=-1.0, in1=rstd[:], op0=ALU.mult, op1=ALU.mult
        )

        gb_ps = auxp.tile([P, 4, P], BF16, name="gb_ps", tag="aux")
        for t in range(4):
            nc.tensor.transpose(gb_ps[:, t, :], rows_s[:, t, :], ident_b[:])
        gb = const.tile([P, 10, 4], F32, name="gb")
        nc.vector.tensor_copy(out=gb[:], in_=gb_ps[:, :, 0:10].rearrange("p t j -> p j t"))

        def bias_chunk(c):
            pb = auxp.tile([P, NB], F32, name="pb", tag="aux")
            nc.tensor.matmul(
                pb[:], lhsT=ident_b[:, c : c + 1].to_broadcast([P, P]), rhs=rows[:], start=True, stop=True
            )
            if c < 10:
                nc.scalar.copy(
                    out=q_sb[:, 256 * c : 256 * (c + 1)],
                    in_=pb[:].rearrange("n (i two) -> n two i", two=2)[:, 0, :],
                )
                nc.scalar.copy(
                    out=ks[:, c // 2, :, 64 * (c % 2) : 64 * (c % 2) + 64],
                    in_=pb[:].rearrange("n (pp e two) -> n two e pp", e=4, two=2)[:, 1],
                )
            else:
                nc.scalar.copy(out=v_sb[:, NB * (c - 10) : NB * (c - 9)], in_=pb[:])

        xc = xpool.tile([P, G, P], U32, name="xc", align_bytes=256)
        xs = xpool.tile([P, G, 2 * P], U8, name="xs", align_bytes=256)

        def x_rows(g):
            xh = xpool.tile([P, 4, P], F32, name="xh", tag="xh", bufs=3)
            nc.scalar.activation(
                out=xh[:],
                in_=inp_sb[:, NB * g : NB * (g + 1)].rearrange("n (p t) -> n t p", t=4),
                func=ACT.Identity,
                scale=rstd[:, 0:1],
                bias=nmr[:, 0:1],
            )
            xt = auxp.tile([P, 4, P], F32, name="xt", tag="aux")
            for t in range(4):
                nc.tensor.transpose(xt[:, t, :], xh[:, t, :], ident_f[:])
            grouped = xpool.tile([P, P, 4], BF16, name="grouped", tag="grouped", bufs=3, align_bytes=64)
            for t in range(4):
                nc.vector.tensor_scalar(
                    out=grouped[:, :, t],
                    in0=xt[:, t, :],
                    scalar1=gb[:, g, t : t + 1],
                    scalar2=gb[:, 5 + g, t : t + 1],
                    op0=ALU.mult,
                    op1=ALU.add,
                )
            return grouped

        def x_quantise(g, grouped):
            nc.vector.quantize_mx(
                out=xc[:, g, :].bitcast(FP8X4),
                scales=xs[:, g, 0:P],
                in_=grouped[:].rearrange("p n t -> p (n t)"),
            )

        grouped = x_rows(0)
        for g in range(1, G):
            ahead = x_rows(g)
            x_quantise(g - 1, grouped)
            grouped = ahead
        x_quantise(G - 1, grouped)

        for c in range(3 * BANKS):
            bias_chunk(c)

        q_dram = out_0[0].rearrange("h n j -> n h j")
        k_dram = out_1.rearrange("o h j n -> (o h j n)").rearrange("(H p f) -> p H f", p=P, f=NB)
        v_dram = out_2[0].rearrange("h n j -> n h j")

        def k_turn(H):
            kt = auxp.tile([P, 4, P], F32, name="kt", tag="aux")
            for e in range(4):
                nc.tensor.transpose(kt[:, e, :], ks[:, H, e, :], ident_f[:])
            nc.scalar.copy(out=k2[:, H, :], in_=kt[:].rearrange("p e n -> p (e n)"))
            nc.sync.dma_start(out=k_dram[:, H, :], in_=k2[:, H, :])

        after = {(1, 0): 0, (1, 1): 1, (2, 0): 2, (2, 1): 3, (2, 2): 4}

        for r in range(3):
            accs = [accp.tile([P, NB], F32, name="acc%d" % b, tag="acc%d" % b) for b in range(BANKS)]
            for g in range(G):
                if g < 4:
                    plane = planes[4 * g : P, RW * r : RW * (r + 1)]
                elif r < 2:
                    plane = planes[4 * r : P, 3 * RW : 4 * RW]
                else:
                    plane = planes_v4[:]
                for b in range(BANKS):
                    nc.tensor.matmul_mx(
                        out=accs[b][:],
                        lhsT=xc[:, g, :].bitcast(FP8X4),
                        lhsT_scale=xs[:, g, 0:P],
                        rhs=words[r][g][:, NB * b : NB * (b + 1)].bitcast(FP8X4),
                        rhs_scale=plane[:, NB * b : NB * (b + 1)],
                        start=(g == 0),
                        stop=(g == G - 1),
                    )
                if (r, g) in after:
                    k_turn(after[r, g])
                if r > 0 and g == 2:
                    nc.sync.dma_start(
                        out=q_dram[:, 10 * (r - 1) : 10 * r, :],
                        in_=q_sb[:, 1280 * (r - 1) : 1280 * r].rearrange("n (h j) -> n h j", j=P),
                    )
            for b in range(BANKS):
                acc = accs[b]
                if r < 2:
                    B = BANKS * r + b
                    q_sl = q_sb[:, 256 * B : 256 * (B + 1)]
                    nc.vector.tensor_tensor(
                        out=q_sl, in0=acc[:].rearrange("n (i two) -> n two i", two=2)[:, 0, :], in1=q_sl, op=ALU.add
                    )
                    k_sl = ks[:, B // 2, :, 64 * (B % 2) : 64 * (B % 2) + 64]
                    nc.vector.tensor_tensor(
                        out=k_sl,
                        in0=acc[:].rearrange("n (pp e two) -> n two e pp", e=4, two=2)[:, 1],
                        in1=k_sl,
                        op=ALU.add,
                    )
                else:
                    v_sl = v_sb[:, NB * b : NB * (b + 1)]
                    nc.vector.tensor_tensor(out=v_sl, in0=acc[:], in1=v_sl, op=ALU.add)
                    nc.sync.dma_start(
                        out=v_dram[:, 4 * b : 4 * (b + 1), :], in_=v_sl.rearrange("n (h j) -> n h j", j=P)
                    )
